import numpy as np
import ml_dtypes


def mxq(x, axis, fmt="e4m3"):
    dtype, down = {"e4m3": (ml_dtypes.float8_e4m3fn, 7), "e5m2": (ml_dtypes.float8_e5m2, 14)}[fmt]
    v = np.moveaxis(np.asarray(x, np.float32).astype(ml_dtypes.bfloat16).astype(np.float64), axis, -1)
    blocks = v.reshape(v.shape[:-1] + (-1, 32))
    amax = np.abs(blocks).max(-1, keepdims=True)
    byte = np.maximum(np.where(amax > 0, np.frexp(amax)[1] - 1 + 127, 0) - down, 1)
    scale = np.exp2(byte - 127.0)
    codes = (blocks / scale).astype(np.float32).astype(dtype).astype(np.float64)
    return np.moveaxis((codes * scale).reshape(v.shape), -1, axis)


WIDE = False


def mx_kscale(k):
    if not WIDE:
        return np.ones(k)
    levels = np.array([10, -10, 5, -5, 0])
    a = np.random.permutation(np.resize(levels, k // 512 * 4)).reshape(k // 512, 4)
    idx = np.arange(k)
    return np.exp2(a[idx // 512, idx % 128 // 32])


BF16 = ml_dtypes.bfloat16


def bf(x):
    return np.asarray(x, np.float32).astype(BF16)


def f64(x):
    return np.asarray(x).astype(np.float64)


E2M1 = np.array([0.0, 0.5, 1.0, 1.5, 2.0, 3.0, 4.0, 6.0, -0.0, -0.5, -1.0, -1.5, -2.0, -3.0, -4.0, -6.0])


def pack_weight(w, fmt):
    k, n = w.shape
    w = f64(bf(w)).reshape(k // 32, 32, n)
    amax = np.abs(w).max(1)
    if fmt == "e4m3":
        byte = np.frexp(amax)[1] - 1 + 127 - 7
    else:
        mant, ex = np.frexp(amax / 6.0)
        byte = np.where(mant > 0.5, ex, ex - 1) + 127
    byte = np.clip(np.where(amax > 0, byte, 1), 1, 254)
    scaled = (w * np.exp2(127.0 - byte)[:, None, :]).reshape(k, n).astype(np.float32)
    by_word = np.ascontiguousarray(scaled.reshape(k // 512, 128, 4, n).transpose(0, 1, 3, 2))
    if fmt == "e4m3":
        words = by_word.astype(ml_dtypes.float8_e4m3fn).view(np.uint8)
    else:
        c = by_word.astype(ml_dtypes.float4_e2m1fn).view(np.uint8) & 0xF
        words = c[..., 0::2] | (c[..., 1::2] << 4)
    return np.ascontiguousarray(words), np.ascontiguousarray(byte.astype(np.uint8).reshape(k // 512, 16, n))


def unpack_weight(words, scales, fmt):
    g, p, n, _ = words.shape
    if fmt == "e4m3":
        vals = np.ascontiguousarray(words).view(ml_dtypes.float8_e4m3fn).astype(np.float64)
    else:
        nib = np.empty((g, p, n, 4), np.uint8)
        nib[..., 0::2] = words & 0xF
        nib[..., 1::2] = words >> 4
        vals = E2M1[nib]
    vals = vals * np.repeat(np.exp2(scales.astype(np.float64) - 127.0), 8, axis=1)[..., None]
    return vals.transpose(0, 1, 3, 2).reshape(g * 512, n)

def pack4(w):
    words, scales = pack_weight(w, "e2m1")
    return words.reshape(words.shape[0], 128, -1), scales


def unpack4(words, scales):
    return unpack_weight(words.reshape(words.shape[0], 128, -1, 2), scales, "e2m1")


N, G, GIN, GOUT = 4096, 2, 1024, 512

P0 = np.array([0.5, 1.0, 0.5, 0.3])
Q0 = np.array([0.5, 0.3, 0.2])


def rational(y, p, q):
    p = p[None, :, :, None]
    q = q[None, :, :, None]
    y2 = y * y
    y3 = y2 * y
    num = p[:, :, 0] + p[:, :, 1] * y + p[:, :, 2] * y2 + p[:, :, 3] * y3
    den = 1.0 + np.abs(q[:, :, 0] * y + q[:, :, 1] * y2 + q[:, :, 2] * y3)
    return num / den


def setup_inputs():
    s = mx_kscale(GIN)
    x = bf(np.random.standard_normal((N, G * GIN)) * np.tile(s, G))
    stack = np.random.standard_normal((G, GIN, GOUT)) / np.sqrt(GIN) / s[None, :, None]
    W_words, W_scales = pack4(stack.reshape(-1, GOUT))
    return {"x": x,
            "W_words": W_words,
            "W_scales": W_scales,
            "b": bf(np.random.standard_normal((G, GOUT)) * 0.3),
            "p": bf(P0 + 0.1 * np.random.standard_normal((G, P0.size))),
            "q": bf(Q0 + 0.05 * np.random.standard_normal((G, Q0.size)))}


def reference(x, W_words, W_scales, b, p, q):
    n = x.shape[0]
    xg = f64(x).reshape(n, G, GIN)
    xq = mxq(xg, 2, "e4m3")
    wq = unpack4(W_words, W_scales).reshape(G, GIN, GOUT)
    y = (xq.transpose(1, 0, 2) @ wq).transpose(1, 0, 2) + f64(b)[None]
    out = rational(y, f64(p), f64(q))
    return out.reshape(n, G * GOUT)

@@ -1,0 +1,234 @@
+from contextlib import ExitStack
+
+import concourse.mybir as mybir
+from concourse.masks import make_identity
+
+F32 = mybir.dt.float32
+BF16 = mybir.dt.bfloat16
+I32 = mybir.dt.int32
+U32 = mybir.dt.uint32
+U8 = mybir.dt.uint8
+FP8X4 = mybir.dt.float8_e4m3fn_x4
+FP4X4 = mybir.dt.float4_e2m1fn_x4
+ALU = mybir.AluOpType
+ACT = mybir.ActivationFunctionType
+
+P = 128
+ROWS = 4096
+GROUPS = 2
+GIN = 1024
+GOUT = 512
+K_PASS = 512
+PASSES = GIN // K_PASS
+WORDS_PASS = K_PASS // 2
+ROW_BLOCKS = ROWS // P
+TILES = ROW_BLOCKS * GROUPS
+LOADS_AHEAD = 4
+
+FLOPS = 2 * ROWS * GROUPS * GIN * GOUT
+
+
+def tile_groupkanlayer_t_e_kernel(tc, x, W_words, W_scales, b, p, q, out):
+    nc = tc.nc
+    with ExitStack() as stack:
+        stack.enter_context(tc.manual_schedule())
+        const = stack.enter_context(tc.tile_pool(name="const", bufs=1))
+        work = stack.enter_context(tc.tile_pool(name="work", bufs=3))
+        psum = stack.enter_context(tc.psum_pool(name="psum", bufs=3))
+
+        x_rows = {}
+
+        def load_x(block):
+            x_sb = work.tile([P, GROUPS * GIN], BF16, name="x_sb", bufs=LOADS_AHEAD + 2)
+            nc.sync.dma_start(out=x_sb[:], in_=x[block * P : (block + 1) * P, :])
+            x_rows[block] = x_sb
+
+        load_x(0)
+        load_x(1)
+
+        w_words = const.tile([P, GROUPS * PASSES, 2 * GOUT], U8, align_bytes=64)
+        nc.sync.dma_start(
+            out=w_words[:].bitcast(I32),
+            in_=W_words.bitcast(I32).rearrange("c p n -> p c n"),
+        )
+        w_planes = const.tile([P, GROUPS * PASSES, GOUT], U8, align_bytes=64)
+        nc.vector.memset(w_planes[:].bitcast(I32), 0)
+        for quadrant in range(4):
+            nc.sync.dma_start(
+                out=w_planes[32 * quadrant : 32 * quadrant + 4].bitcast(I32),
+                in_=W_scales.bitcast(I32)[:, 4 * quadrant : 4 * quadrant + 4, :].rearrange(
+                    "c r n -> r c n"
+                ),
+            )
+
+        bias_bf = const.tile([P, GROUPS * GOUT], BF16)
+        nc.sync.dma_start(out=bias_bf[:], in_=b.rearrange("g o -> (g o)").partition_broadcast(P))
+        bias = const.tile([P, GROUPS * GOUT], F32)
+        nc.vector.tensor_copy(out=bias[:], in_=bias_bf[:])
+
+        p_bf = const.tile([P, GROUPS * 4], BF16)
+        nc.sync.dma_start(out=p_bf[:], in_=p.rearrange("g c -> (g c)").partition_broadcast(P))
+        p_f32 = const.tile([P, GROUPS * 4], F32)
+        nc.vector.tensor_copy(out=p_f32[:], in_=p_bf[:])
+        q_bf = const.tile([P, GROUPS * 3], BF16)
+        nc.sync.dma_start(out=q_bf[:], in_=q.rearrange("g c -> (g c)").partition_broadcast(P))
+        q_f32 = const.tile([P, GROUPS * 3], F32)
+        nc.vector.tensor_copy(out=q_f32[:], in_=q_bf[:])
+
+        def p_coef(g, power):
+            return p_f32[:, 4 * g + power : 4 * g + power + 1]
+
+        def q_coef(g, power):
+            return q_f32[:, 3 * g + power - 1 : 3 * g + power]
+
+        one = const.tile([P, 1], F32)
+        nc.vector.memset(one[:], 1.0)
+
+        ident = const.tile([P, P], F32)
+        make_identity(nc, ident[:])
+
+        for block in range(2, LOADS_AHEAD):
+            load_x(block)
+
+        turned = {}
+        grouped = {}
+        x_codes = {}
+        x_scales = {}
+        sums = {}
+        ys = {}
+        num = {}
+        den = {}
+
+        def turn_x(i):
+            block, g = divmod(i, GROUPS)
+            x_words = x_rows[block][:].bitcast(F32)
+            xt = psum.tile([P, PASSES, 2, P], F32, name="xt")
+            for c in range(PASSES):
+                first = (g * PASSES + c) * WORDS_PASS
+                for u in range(2):
+                    nc.tensor.transpose(
+                        xt[:, c, u, :], x_words[:, first + u : first + WORDS_PASS : 2], ident[:]
+                    )
+            turned[i] = xt
+
+        def group_x(i):
+            gx = work.tile([P, PASSES * P * 4], BF16, name="gx", align_bytes=64)
+            nc.scalar.copy(
+                out=gx[:].bitcast(F32).rearrange("p (c n u) -> p c n u", c=PASSES, u=2),
+                in_=turned[i][:].rearrange("p c u n -> p c n u"),
+            )
+            grouped[i] = gx
+
+        def quantise_x(i):
+            codes = work.tile([P, PASSES * P], U32, name="codes", align_bytes=64)
+            scales = work.tile([P, PASSES * P], U8, name="scales", align_bytes=64)
+            nc.vector.quantize_mx(out=codes[:].bitcast(FP8X4), scales=scales[:], in_=grouped[i][:])
+            x_codes[i] = codes
+            x_scales[i] = scales
+
+        def multiply(i):
+            g = i % GROUPS
+            acc = psum.tile([P, GOUT], F32, name="acc")
+            for c in range(PASSES):
+                rows = slice(c * P, (c + 1) * P)
+                nc.tensor.matmul_mx(
+                    out=acc[:],
+                    lhsT=x_codes[i][:, rows].bitcast(FP8X4),
+                    lhsT_scale=x_scales[i][:, rows],
+                    rhs=w_words[:, g * PASSES + c, :].bitcast(FP4X4),
+                    rhs_scale=w_planes[:, g * PASSES + c, :],
+                    start=(c == 0),
+                    stop=(c == PASSES - 1),
+                )
+            sums[i] = acc
+
+        def add_bias(i):
+            g = i % GROUPS
+            y = work.tile([P, GOUT], F32, name="y", bufs=6)
+            nc.vector.tensor_tensor(
+                out=y[:], in0=sums[i][:], in1=bias[:, g * GOUT : (g + 1) * GOUT], op=ALU.add
+            )
+            ys[i] = y
+
+        def horner_first(i):
+            g = i % GROUPS
+            n1 = work.tile([P, GOUT], F32, name="n1")
+            nc.scalar.activation(
+                out=n1[:], in_=ys[i][:], func=ACT.Identity, scale=p_coef(g, 3), bias=p_coef(g, 2)
+            )
+            d1 = work.tile([P, GOUT], F32, name="d1")
+            nc.scalar.activation(
+                out=d1[:], in_=ys[i][:], func=ACT.Identity, scale=q_coef(g, 3), bias=q_coef(g, 2)
+            )
+            num[i] = n1
+            den[i] = d1
+
+        def horner_second(i):
+            n2 = work.tile([P, GOUT], F32, name="n2")
+            nc.vector.tensor_tensor(out=n2[:], in0=num[i][:], in1=ys[i][:], op=ALU.mult)
+            d2 = work.tile([P, GOUT], F32, name="d2")
+            nc.vector.tensor_tensor(out=d2[:], in0=den[i][:], in1=ys[i][:], op=ALU.mult)
+            num[i] = n2
+            den[i] = d2
+
+        def horner_third(i):
+            g = i % GROUPS
+            n3 = work.tile([P, GOUT], F32, name="n3", bufs=7)
+            nc.vector.scalar_tensor_tensor(
+                out=n3[:], in0=num[i][:], scalar=p_coef(g, 1), in1=ys[i][:], op0=ALU.add, op1=ALU.mult
+            )
+            d3 = work.tile([P, GOUT], F32, name="d3")
+            nc.vector.scalar_tensor_tensor(
+                out=d3[:], in0=den[i][:], scalar=q_coef(g, 1), in1=ys[i][:], op0=ALU.add, op1=ALU.mult
+            )
+            num[i] = n3
+            den[i] = d3
+
+        def magnitude(i):
+            d4 = work.tile([P, GOUT], F32, name="d4")
+            nc.scalar.activation(out=d4[:], in_=den[i][:], func=ACT.Abs)
+            den[i] = d4
+
+        def inverse_root(i):
+            d5 = work.tile([P, GOUT], F32, name="d5")
+            nc.scalar.activation(
+                out=d5[:], in_=den[i][:], func=ACT.Abs_reciprocal_sqrt, bias=one[:]
+            )
+            den[i] = d5
+
+        def inverse(i):
+            d6 = work.tile([P, GOUT], F32, name="d6")
+            nc.scalar.activation(out=d6[:], in_=den[i][:], func=ACT.Square)
+            den[i] = d6
+
+        def divide_and_store(i):
+            block, g = divmod(i, GROUPS)
+            res = work.tile([P, GOUT], F32, name="res", bufs=4)
+            nc.vector.scalar_tensor_tensor(
+                out=res[:], in0=num[i][:], scalar=p_coef(g, 0), in1=den[i][:], op0=ALU.add, op1=ALU.mult
+            )
+            nc.sync.dma_start(
+                out=out[block * P : (block + 1) * P, g * GOUT : (g + 1) * GOUT], in_=res[:]
+            )
+
+        def run(stage, i):
+            if 0 <= i < TILES:
+                stage(i)
+
+        LAST_LAG = 11
+        for step in range(TILES + LAST_LAG):
+            next_block = step // GROUPS + LOADS_AHEAD
+            if step % GROUPS == 0 and next_block < ROW_BLOCKS:
+                load_x(next_block)
+            run(turn_x, step)
+            run(group_x, step - 1)
+            run(quantise_x, step - 2)
+            run(multiply, step - 3)
+            run(add_bias, step - 4)
+            run(horner_first, step - 5)
+            run(horner_second, step - 6)
+            run(horner_third, step - 7)
+            run(magnitude, step - 8)
+            run(inverse_root, step - 9)
+            run(inverse, step - 10)
+            run(divide_and_store, step - LAST_LAG)

@@ -23,7 +23,7 @@ PASSES = GIN // K_PASS
 WORDS_PASS = K_PASS // 2
 ROW_BLOCKS = ROWS // P
 TILES = ROW_BLOCKS * GROUPS
-LOADS_AHEAD = 4
+LOADS_AHEAD = 8
 
 FLOPS = 2 * ROWS * GROUPS * GIN * GOUT
 
@@ -36,12 +36,15 @@ def tile_groupkanlayer_t_e_kernel(tc, x, W_words, W_scales, b, p, q, out):
         work = stack.enter_context(tc.tile_pool(name="work", bufs=3))
         psum = stack.enter_context(tc.psum_pool(name="psum", bufs=3))
 
-        x_rows = {}
+        x_part = {}
 
-        def load_x(block):
-            x_sb = work.tile([P, GROUPS * GIN], BF16, name="x_sb", bufs=LOADS_AHEAD + 2)
-            nc.sync.dma_start(out=x_sb[:], in_=x[block * P : (block + 1) * P, :])
-            x_rows[block] = x_sb
+        def load_x(i):
+            block, g = divmod(i, GROUPS)
+            x_sb = work.tile([P, GIN], BF16, name="x_sb", bufs=LOADS_AHEAD + 2)
+            nc.sync.dma_start(
+                out=x_sb[:], in_=x[block * P : (block + 1) * P, g * GIN : (g + 1) * GIN]
+            )
+            x_part[i] = x_sb
 
         load_x(0)
         load_x(1)
@@ -87,8 +90,8 @@ def tile_groupkanlayer_t_e_kernel(tc, x, W_words, W_scales, b, p, q, out):
         ident = const.tile([P, P], F32)
         make_identity(nc, ident[:])
 
-        for block in range(2, LOADS_AHEAD):
-            load_x(block)
+        for i in range(2, LOADS_AHEAD):
+            load_x(i)
 
         turned = {}
         grouped = {}
@@ -96,15 +99,15 @@ def tile_groupkanlayer_t_e_kernel(tc, x, W_words, W_scales, b, p, q, out):
         x_scales = {}
         sums = {}
         ys = {}
+        both = {}
         num = {}
         den = {}
 
         def turn_x(i):
-            block, g = divmod(i, GROUPS)
-            x_words = x_rows[block][:].bitcast(F32)
+            x_words = x_part[i][:].bitcast(F32)
             xt = psum.tile([P, PASSES, 2, P], F32, name="xt")
             for c in range(PASSES):
-                first = (g * PASSES + c) * WORDS_PASS
+                first = c * WORDS_PASS
                 for u in range(2):
                     nc.tensor.transpose(
                         xt[:, c, u, :], x_words[:, first + u : first + WORDS_PASS : 2], ident[:]
@@ -152,34 +155,34 @@ def tile_groupkanlayer_t_e_kernel(tc, x, W_words, W_scales, b, p, q, out):
 
         def horner_first(i):
             g = i % GROUPS
-            n1 = work.tile([P, GOUT], F32, name="n1")
+            nd1 = work.tile([P, 2, GOUT], F32, name="nd1")
             nc.scalar.activation(
-                out=n1[:], in_=ys[i][:], func=ACT.Identity, scale=p_coef(g, 3), bias=p_coef(g, 2)
+                out=nd1[:, 0, :], in_=ys[i][:], func=ACT.Identity, scale=p_coef(g, 3), bias=p_coef(g, 2)
             )
-            d1 = work.tile([P, GOUT], F32, name="d1")
             nc.scalar.activation(
-                out=d1[:], in_=ys[i][:], func=ACT.Identity, scale=q_coef(g, 3), bias=q_coef(g, 2)
+                out=nd1[:, 1, :], in_=ys[i][:], func=ACT.Identity, scale=q_coef(g, 3), bias=q_coef(g, 2)
             )
-            num[i] = n1
-            den[i] = d1
+            both[i] = nd1
 
         def horner_second(i):
-            n2 = work.tile([P, GOUT], F32, name="n2")
-            nc.vector.tensor_tensor(out=n2[:], in0=num[i][:], in1=ys[i][:], op=ALU.mult)
-            d2 = work.tile([P, GOUT], F32, name="d2")
-            nc.vector.tensor_tensor(out=d2[:], in0=den[i][:], in1=ys[i][:], op=ALU.mult)
-            num[i] = n2
-            den[i] = d2
+            nd2 = work.tile([P, 2, GOUT], F32, name="nd2")
+            nc.vector.tensor_tensor(
+                out=nd2[:],
+                in0=both[i][:],
+                in1=ys[i][:].unsqueeze(1).to_broadcast([P, 2, GOUT]),
+                op=ALU.mult,
+            )
+            both[i] = nd2
 
         def horner_third(i):
             g = i % GROUPS
             n3 = work.tile([P, GOUT], F32, name="n3", bufs=7)
             nc.vector.scalar_tensor_tensor(
-                out=n3[:], in0=num[i][:], scalar=p_coef(g, 1), in1=ys[i][:], op0=ALU.add, op1=ALU.mult
+                out=n3[:], in0=both[i][:, 0, :], scalar=p_coef(g, 1), in1=ys[i][:], op0=ALU.add, op1=ALU.mult
             )
             d3 = work.tile([P, GOUT], F32, name="d3")
             nc.vector.scalar_tensor_tensor(
-                out=d3[:], in0=den[i][:], scalar=q_coef(g, 1), in1=ys[i][:], op0=ALU.add, op1=ALU.mult
+                out=d3[:], in0=both[i][:, 1, :], scalar=q_coef(g, 1), in1=ys[i][:], op0=ALU.add, op1=ALU.mult
             )
             num[i] = n3
             den[i] = d3
@@ -217,18 +220,16 @@ def tile_groupkanlayer_t_e_kernel(tc, x, W_words, W_scales, b, p, q, out):
 
         LAST_LAG = 11
         for step in range(TILES + LAST_LAG):
-            next_block = step // GROUPS + LOADS_AHEAD
-            if step % GROUPS == 0 and next_block < ROW_BLOCKS:
-                load_x(next_block)
-            run(turn_x, step)
-            run(group_x, step - 1)
-            run(quantise_x, step - 2)
-            run(multiply, step - 3)
-            run(add_bias, step - 4)
-            run(horner_first, step - 5)
-            run(horner_second, step - 6)
-            run(horner_third, step - 7)
-            run(magnitude, step - 8)
-            run(inverse_root, step - 9)
-            run(inverse, step - 10)
             run(divide_and_store, step - LAST_LAG)
+            run(inverse, step - 10)
+            run(inverse_root, step - 9)
+            run(magnitude, step - 8)
+            run(horner_third, step - 7)
+            run(horner_second, step - 6)
+            run(horner_first, step - 5)
+            run(add_bias, step - 4)
+            run(multiply, step - 3)
+            run(quantise_x, step - 2)
+            run(group_x, step - 1)
+            run(turn_x, step)
+            run(load_x, step + LOADS_AHEAD)

@@ -21,9 +21,14 @@ GOUT = 512
 K_PASS = 512
 PASSES = GIN // K_PASS
 WORDS_PASS = K_PASS // 2
-ROW_BLOCKS = ROWS // P
-TILES = ROW_BLOCKS * GROUPS
+NB = 512
+SUB = NB // P
+OBS = GOUT // P
+MACROS = (ROWS // NB) * GROUPS
+TILES = MACROS * OBS
+UNITS = MACROS * SUB
 LOADS_AHEAD = 8
+SQUARE_ON_GPSIMD = False
 
 FLOPS = 2 * ROWS * GROUPS * GIN * GOUT
 
@@ -34,20 +39,20 @@ def tile_groupkanlayer_t_e_kernel(tc, x, W_words, W_scales, b, p, q, out):
         stack.enter_context(tc.manual_schedule())
         const = stack.enter_context(tc.tile_pool(name="const", bufs=1))
         work = stack.enter_context(tc.tile_pool(name="work", bufs=3))
-        psum = stack.enter_context(tc.psum_pool(name="psum", bufs=3))
+        psum = stack.enter_context(tc.psum_pool(name="psum", bufs=2))
 
         x_part = {}
 
-        def load_x(i):
-            block, g = divmod(i, GROUPS)
+        def load_x(u):
+            m, r = divmod(u, SUB)
+            nb, g = divmod(m, GROUPS)
             x_sb = work.tile([P, GIN], BF16, name="x_sb", bufs=LOADS_AHEAD + 2)
-            nc.sync.dma_start(
-                out=x_sb[:], in_=x[block * P : (block + 1) * P, g * GIN : (g + 1) * GIN]
-            )
-            x_part[i] = x_sb
+            row0 = nb * NB + r * P
+            nc.sync.dma_start(out=x_sb[:], in_=x[row0 : row0 + P, g * GIN : (g + 1) * GIN])
+            x_part[u] = x_sb
 
-        load_x(0)
-        load_x(1)
+        for u in range(4):
+            load_x(u)
 
         w_words = const.tile([P, GROUPS * PASSES, 2 * GOUT], U8, align_bytes=64)
         nc.sync.dma_start(
@@ -64,10 +69,20 @@ def tile_groupkanlayer_t_e_kernel(tc, x, W_words, W_scales, b, p, q, out):
                 ),
             )
 
-        bias_bf = const.tile([P, GROUPS * GOUT], BF16)
-        nc.sync.dma_start(out=bias_bf[:], in_=b.rearrange("g o -> (g o)").partition_broadcast(P))
-        bias = const.tile([P, GROUPS * GOUT], F32)
-        nc.vector.tensor_copy(out=bias[:], in_=bias_bf[:])
+        ident = const.tile([P, P], F32)
+        make_identity(nc, ident[:])
+
+        b_rows_bf = const.tile([P, P], BF16)
+        nc.vector.memset(b_rows_bf[:], 0.0)
+        nc.sync.dma_start(
+            out=b_rows_bf[0 : GROUPS * OBS, :], in_=b.rearrange("g (k c) -> (g k) c", c=P)
+        )
+        b_rows = const.tile([P, P], F32)
+        nc.vector.tensor_copy(out=b_rows[:], in_=b_rows_bf[:])
+        b_turned = psum.tile([P, SUB, P], F32, name="nt")
+        nc.tensor.transpose(b_turned[:, 0, :], b_rows[:], ident[:])
+        b_col = const.tile([P, GROUPS * OBS], F32)
+        nc.vector.tensor_copy(out=b_col[:], in_=b_turned[:, 0, 0 : GROUPS * OBS])
 
         p_bf = const.tile([P, GROUPS * 4], BF16)
         nc.sync.dma_start(out=p_bf[:], in_=p.rearrange("g c -> (g c)").partition_broadcast(P))
@@ -87,149 +102,204 @@ def tile_groupkanlayer_t_e_kernel(tc, x, W_words, W_scales, b, p, q, out):
         one = const.tile([P, 1], F32)
         nc.vector.memset(one[:], 1.0)
 
-        ident = const.tile([P, P], F32)
-        make_identity(nc, ident[:])
+        mid_const_p = const.tile([P, GROUPS * OBS], F32)
+        mid_const_q = const.tile([P, GROUPS * OBS], F32)
+        for g in range(GROUPS):
+            cols = slice(g * OBS, (g + 1) * OBS)
+            nc.vector.tensor_scalar(
+                out=mid_const_p[:, cols], in0=b_col[:, cols], scalar1=p_coef(g, 2),
+                scalar2=p_coef(g, 1), op0=ALU.mult, op1=ALU.add,
+            )
+            nc.vector.tensor_scalar(
+                out=mid_const_q[:, cols], in0=b_col[:, cols], scalar1=q_coef(g, 2),
+                scalar2=q_coef(g, 1), op0=ALU.mult, op1=ALU.add,
+            )
 
-        for i in range(2, LOADS_AHEAD):
-            load_x(i)
+        for u in range(4, LOADS_AHEAD):
+            load_x(u)
 
         turned = {}
         grouped = {}
         x_codes = {}
         x_scales = {}
         sums = {}
-        ys = {}
-        both = {}
-        num = {}
+        first = {}
+        prod1 = {}
+        plus1 = {}
+        prod2 = {}
+        q_back = {}
+        n_back = {}
         den = {}
 
-        def turn_x(i):
-            x_words = x_part[i][:].bitcast(F32)
+        def where(i):
+            m, ob = divmod(i, OBS)
+            nb, g = divmod(m, GROUPS)
+            return nb, g, ob
+
+        def turn_x(u):
+            x_words = x_part[u][:].bitcast(F32)
             xt = psum.tile([P, PASSES, 2, P], F32, name="xt")
             for c in range(PASSES):
-                first = c * WORDS_PASS
-                for u in range(2):
+                w0 = c * WORDS_PASS
+                for h in range(2):
                     nc.tensor.transpose(
-                        xt[:, c, u, :], x_words[:, first + u : first + WORDS_PASS : 2], ident[:]
+                        xt[:, c, h, :], x_words[:, w0 + h : w0 + WORDS_PASS : 2], ident[:]
                     )
-            turned[i] = xt
+            turned[u] = xt
 
-        def group_x(i):
-            gx = work.tile([P, PASSES * P * 4], BF16, name="gx", align_bytes=64)
+        def group_x(u):
+            m, r = divmod(u, SUB)
+            if r == 0:
+                gx_new = work.tile([P, PASSES * NB * 4], BF16, name="gx", bufs=2, align_bytes=64)
+                grouped[m] = gx_new
+            gx = grouped[m]
             nc.scalar.copy(
-                out=gx[:].bitcast(F32).rearrange("p (c n u) -> p c n u", c=PASSES, u=2),
-                in_=turned[i][:].rearrange("p c u n -> p c n u"),
+                out=gx[:].bitcast(F32).rearrange("p (c n h) -> p c n h", c=PASSES, h=2)[
+                    :, :, r * P : (r + 1) * P, :
+                ],
+                in_=turned[u][:].rearrange("p c h n -> p c n h"),
             )
-            grouped[i] = gx
 
-        def quantise_x(i):
-            codes = work.tile([P, PASSES * P], U32, name="codes", align_bytes=64)
-            scales = work.tile([P, PASSES * P], U8, name="scales", align_bytes=64)
-            nc.vector.quantize_mx(out=codes[:].bitcast(FP8X4), scales=scales[:], in_=grouped[i][:])
-            x_codes[i] = codes
-            x_scales[i] = scales
+        def quantise_x(m):
+            codes = work.tile([P, PASSES * NB], U32, name="codes", bufs=2, align_bytes=64)
+            scales = work.tile([P, PASSES * NB], U8, name="scales", bufs=2, align_bytes=64)
+            nc.vector.quantize_mx(out=codes[:].bitcast(FP8X4), scales=scales[:], in_=grouped[m][:])
+            x_codes[m] = codes
+            x_scales[m] = scales
 
         def multiply(i):
-            g = i % GROUPS
-            acc = psum.tile([P, GOUT], F32, name="acc")
+            nb, g, ob = where(i)
+            m = i // OBS
+            acc = psum.tile([P, NB], F32, name="acc", bufs=3)
             for c in range(PASSES):
-                rows = slice(c * P, (c + 1) * P)
+                cols = slice(c * NB, (c + 1) * NB)
                 nc.tensor.matmul_mx(
                     out=acc[:],
-                    lhsT=x_codes[i][:, rows].bitcast(FP8X4),
-                    lhsT_scale=x_scales[i][:, rows],
-                    rhs=w_words[:, g * PASSES + c, :].bitcast(FP4X4),
-                    rhs_scale=w_planes[:, g * PASSES + c, :],
+                    lhsT=w_words[:, g * PASSES + c, ob * 2 * P : (ob + 1) * 2 * P].bitcast(FP4X4),
+                    lhsT_scale=w_planes[:, g * PASSES + c, ob * P : (ob + 1) * P],
+                    rhs=x_codes[m][:, cols].bitcast(FP8X4),
+                    rhs_scale=x_scales[m][:, cols],
                     start=(c == 0),
                     stop=(c == PASSES - 1),
                 )
             sums[i] = acc
 
-        def add_bias(i):
-            g = i % GROUPS
-            y = work.tile([P, GOUT], F32, name="y", bufs=6)
-            nc.vector.tensor_tensor(
-                out=y[:], in0=sums[i][:], in1=bias[:, g * GOUT : (g + 1) * GOUT], op=ALU.add
-            )
-            ys[i] = y
-
-        def horner_first(i):
-            g = i % GROUPS
-            nd1 = work.tile([P, 2, GOUT], F32, name="nd1")
+        def square_y(i):
+            nb, g, ob = where(i)
+            k = g * OBS + ob
+            y2 = work.tile([P, NB], F32, name="y2")
             nc.scalar.activation(
-                out=nd1[:, 0, :], in_=ys[i][:], func=ACT.Identity, scale=p_coef(g, 3), bias=p_coef(g, 2)
+                out=y2[:], in_=sums[i][:], func=ACT.Square, bias=b_col[:, k : k + 1]
             )
-            nc.scalar.activation(
-                out=nd1[:, 1, :], in_=ys[i][:], func=ACT.Identity, scale=q_coef(g, 3), bias=q_coef(g, 2)
-            )
-            both[i] = nd1
+            first[i] = y2
 
-        def horner_second(i):
-            nd2 = work.tile([P, 2, GOUT], F32, name="nd2")
-            nc.vector.tensor_tensor(
-                out=nd2[:],
-                in0=both[i][:],
-                in1=ys[i][:].unsqueeze(1).to_broadcast([P, 2, GOUT]),
-                op=ALU.mult,
+        def outer_terms(i):
+            nb, g, ob = where(i)
+            k = g * OBS + ob
+            e = work.tile([P, 2, NB], F32, name="e")
+            nc.gpsimd.tensor_scalar(
+                out=e[:, 0, :], in0=first[i][:], scalar1=q_coef(g, 3),
+                scalar2=mid_const_q[:, k : k + 1], op0=ALU.mult, op1=ALU.add,
             )
-            both[i] = nd2
+            nc.gpsimd.tensor_scalar(
+                out=e[:, 1, :], in0=first[i][:], scalar1=p_coef(g, 3),
+                scalar2=mid_const_p[:, k : k + 1], op0=ALU.mult, op1=ALU.add,
+            )
+            prod1[i] = e
 
-        def horner_third(i):
-            g = i % GROUPS
-            n3 = work.tile([P, GOUT], F32, name="n3", bufs=7)
+        def quadratics(i):
+            nb, g, ob = where(i)
+            h = work.tile([P, 2, NB], F32, name="h1")
             nc.vector.scalar_tensor_tensor(
-                out=n3[:], in0=both[i][:, 0, :], scalar=p_coef(g, 1), in1=ys[i][:], op0=ALU.add, op1=ALU.mult
+                out=h[:, 0, :], in0=sums[i][:], scalar=q_coef(g, 2), in1=prod1[i][:, 0, :],
+                op0=ALU.mult, op1=ALU.add,
             )
-            d3 = work.tile([P, GOUT], F32, name="d3")
             nc.vector.scalar_tensor_tensor(
-                out=d3[:], in0=both[i][:, 1, :], scalar=q_coef(g, 1), in1=ys[i][:], op0=ALU.add, op1=ALU.mult
+                out=h[:, 1, :], in0=sums[i][:], scalar=p_coef(g, 2), in1=prod1[i][:, 1, :],
+                op0=ALU.mult, op1=ALU.add,
             )
-            num[i] = n3
-            den[i] = d3
+            plus1[i] = h
+
+        def product_two(i):
+            nb, g, ob = where(i)
+            k = g * OBS + ob
+            res = work.tile([P, 2, NB], F32, name="m2")
+            nc.vector.scalar_tensor_tensor(
+                out=res[:],
+                in0=sums[i][:].unsqueeze(1).to_broadcast([P, 2, NB]),
+                scalar=b_col[:, k : k + 1],
+                in1=plus1[i][:],
+                op0=ALU.add,
+                op1=ALU.mult,
+            )
+            prod2[i] = res
+
+        def turn_back(i):
+            qt = psum.tile([P, SUB, P], F32, name="qt", bufs=1)
+            for j in range(SUB):
+                nc.tensor.transpose(qt[:, j, :], prod2[i][:, 0, j * P : (j + 1) * P], ident[:])
+            nt = psum.tile([P, SUB, P], F32, name="nt")
+            for j in range(SUB):
+                nc.tensor.transpose(nt[:, j, :], prod2[i][:, 1, j * P : (j + 1) * P], ident[:])
+            q_back[i] = qt
+            n_back[i] = nt
 
         def magnitude(i):
-            d4 = work.tile([P, GOUT], F32, name="d4")
-            nc.scalar.activation(out=d4[:], in_=den[i][:], func=ACT.Abs)
+            d4 = work.tile([P, NB], F32, name="d4")
+            nc.scalar.activation(
+                out=d4[:], in_=q_back[i][:].rearrange("p j o -> p (j o)"), func=ACT.Abs
+            )
             den[i] = d4
 
         def inverse_root(i):
-            d5 = work.tile([P, GOUT], F32, name="d5")
+            d5 = work.tile([P, NB], F32, name="d5")
             nc.scalar.activation(
                 out=d5[:], in_=den[i][:], func=ACT.Abs_reciprocal_sqrt, bias=one[:]
             )
             den[i] = d5
 
         def inverse(i):
-            d6 = work.tile([P, GOUT], F32, name="d6")
-            nc.scalar.activation(out=d6[:], in_=den[i][:], func=ACT.Square)
+            d6 = work.tile([P, NB], F32, name="d6")
+            if SQUARE_ON_GPSIMD:
+                nc.gpsimd.tensor_tensor(out=d6[:], in0=den[i][:], in1=den[i][:], op=ALU.mult)
+            else:
+                nc.scalar.activation(out=d6[:], in_=den[i][:], func=ACT.Square)
             den[i] = d6
 
         def divide_and_store(i):
-            block, g = divmod(i, GROUPS)
-            res = work.tile([P, GOUT], F32, name="res", bufs=4)
+            nb, g, ob = where(i)
+            res = work.tile([P, SUB, P], F32, name="res", bufs=4)
             nc.vector.scalar_tensor_tensor(
-                out=res[:], in0=num[i][:], scalar=p_coef(g, 0), in1=den[i][:], op0=ALU.add, op1=ALU.mult
+                out=res[:].rearrange("p j o -> p (j o)"),
+                in0=n_back[i][:].rearrange("p j o -> p (j o)"),
+                scalar=p_coef(g, 0),
+                in1=den[i][:],
+                op0=ALU.add,
+                op1=ALU.mult,
             )
+            col0 = g * GOUT + ob * P
             nc.sync.dma_start(
-                out=out[block * P : (block + 1) * P, g * GOUT : (g + 1) * GOUT], in_=res[:]
+                out=out[nb * NB : (nb + 1) * NB, col0 : col0 + P].rearrange("(j r) o -> r j o", r=P),
+                in_=res[:],
             )
 
-        def run(stage, i):
-            if 0 <= i < TILES:
+        def run(stage, i, count=TILES):
+            if 0 <= i < count:
                 stage(i)
 
-        LAST_LAG = 11
-        for step in range(TILES + LAST_LAG):
-            run(divide_and_store, step - LAST_LAG)
-            run(inverse, step - 10)
-            run(inverse_root, step - 9)
-            run(magnitude, step - 8)
-            run(horner_third, step - 7)
-            run(horner_second, step - 6)
-            run(horner_first, step - 5)
-            run(add_bias, step - 4)
-            run(multiply, step - 3)
-            run(quantise_x, step - 2)
-            run(group_x, step - 1)
-            run(turn_x, step)
-            run(load_x, step + LOADS_AHEAD)
+        for t in range(-8, TILES + 3):
+            run(inverse, t - 2)
+            run(square_y, t + 1)
+            run(outer_terms, t + 1)
+            run(quadratics, t)
+            if (t + 3) % OBS == 0:
+                run(quantise_x, (t + 3) // OBS, MACROS)
+            run(divide_and_store, t - 2)
+            run(product_two, t)
+            run(turn_back, t - 1)
+            run(magnitude, t - 1)
+            run(group_x, t + 7, UNITS)
+            run(inverse_root, t - 1)
+            run(turn_x, t + 8, UNITS)
+            run(multiply, t + 2)
+            run(load_x, t + 8 + LOADS_AHEAD, UNITS)

@@ -28,7 +28,8 @@ MACROS = (ROWS // NB) * GROUPS
 TILES = MACROS * OBS
 UNITS = MACROS * SUB
 LOADS_AHEAD = 8
-SQUARE_ON_GPSIMD = False
+SQUARE_ON_GPSIMD = ()
+FINAL_ON_GPSIMD = (3,)
 
 FLOPS = 2 * ROWS * GROUPS * GIN * GOUT
 
@@ -51,6 +52,16 @@ def tile_groupkanlayer_t_e_kernel(tc, x, W_words, W_scales, b, p, q, out):
             nc.sync.dma_start(out=x_sb[:], in_=x[row0 : row0 + P, g * GIN : (g + 1) * GIN])
             x_part[u] = x_sb
 
+        b_rows_bf = const.tile([P, P], BF16)
+        nc.vector.memset(b_rows_bf[:], 0.0)
+        nc.scalar.dma_start(
+            out=b_rows_bf[0 : GROUPS * OBS, :], in_=b.rearrange("g (k c) -> (g k) c", c=P)
+        )
+        p_bf = const.tile([P, GROUPS * 4], BF16)
+        nc.scalar.dma_start(out=p_bf[:], in_=p.rearrange("g c -> (g c)").partition_broadcast(P))
+        q_bf = const.tile([P, GROUPS * 3], BF16)
+        nc.scalar.dma_start(out=q_bf[:], in_=q.rearrange("g c -> (g c)").partition_broadcast(P))
+
         for u in range(4):
             load_x(u)
 
@@ -72,24 +83,11 @@ def tile_groupkanlayer_t_e_kernel(tc, x, W_words, W_scales, b, p, q, out):
         ident = const.tile([P, P], F32)
         make_identity(nc, ident[:])
 
-        b_rows_bf = const.tile([P, P], BF16)
-        nc.vector.memset(b_rows_bf[:], 0.0)
-        nc.sync.dma_start(
-            out=b_rows_bf[0 : GROUPS * OBS, :], in_=b.rearrange("g (k c) -> (g k) c", c=P)
-        )
         b_rows = const.tile([P, P], F32)
         nc.vector.tensor_copy(out=b_rows[:], in_=b_rows_bf[:])
-        b_turned = psum.tile([P, SUB, P], F32, name="nt")
-        nc.tensor.transpose(b_turned[:, 0, :], b_rows[:], ident[:])
         b_col = const.tile([P, GROUPS * OBS], F32)
-        nc.vector.tensor_copy(out=b_col[:], in_=b_turned[:, 0, 0 : GROUPS * OBS])
-
-        p_bf = const.tile([P, GROUPS * 4], BF16)
-        nc.sync.dma_start(out=p_bf[:], in_=p.rearrange("g c -> (g c)").partition_broadcast(P))
         p_f32 = const.tile([P, GROUPS * 4], F32)
         nc.vector.tensor_copy(out=p_f32[:], in_=p_bf[:])
-        q_bf = const.tile([P, GROUPS * 3], BF16)
-        nc.sync.dma_start(out=q_bf[:], in_=q.rearrange("g c -> (g c)").partition_broadcast(P))
         q_f32 = const.tile([P, GROUPS * 3], F32)
         nc.vector.tensor_copy(out=q_f32[:], in_=q_bf[:])
 
@@ -104,16 +102,21 @@ def tile_groupkanlayer_t_e_kernel(tc, x, W_words, W_scales, b, p, q, out):
 
         mid_const_p = const.tile([P, GROUPS * OBS], F32)
         mid_const_q = const.tile([P, GROUPS * OBS], F32)
-        for g in range(GROUPS):
-            cols = slice(g * OBS, (g + 1) * OBS)
-            nc.vector.tensor_scalar(
-                out=mid_const_p[:, cols], in0=b_col[:, cols], scalar1=p_coef(g, 2),
-                scalar2=p_coef(g, 1), op0=ALU.mult, op1=ALU.add,
-            )
-            nc.vector.tensor_scalar(
-                out=mid_const_q[:, cols], in0=b_col[:, cols], scalar1=q_coef(g, 2),
-                scalar2=q_coef(g, 1), op0=ALU.mult, op1=ALU.add,
-            )
+
+        def channel_constants():
+            b_turned = psum.tile([P, SUB, P], F32, name="nt")
+            nc.tensor.transpose(b_turned[:, 0, :], b_rows[:], ident[:])
+            nc.vector.tensor_copy(out=b_col[:], in_=b_turned[:, 0, 0 : GROUPS * OBS])
+            for g in range(GROUPS):
+                cols = slice(g * OBS, (g + 1) * OBS)
+                nc.vector.tensor_scalar(
+                    out=mid_const_p[:, cols], in0=b_col[:, cols], scalar1=p_coef(g, 2),
+                    scalar2=p_coef(g, 1), op0=ALU.mult, op1=ALU.add,
+                )
+                nc.vector.tensor_scalar(
+                    out=mid_const_q[:, cols], in0=b_col[:, cols], scalar1=q_coef(g, 2),
+                    scalar2=q_coef(g, 1), op0=ALU.mult, op1=ALU.add,
+                )
 
         for u in range(4, LOADS_AHEAD):
             load_x(u)
@@ -163,9 +166,22 @@ def tile_groupkanlayer_t_e_kernel(tc, x, W_words, W_scales, b, p, q, out):
         def quantise_x(m):
             codes = work.tile([P, PASSES * NB], U32, name="codes", bufs=2, align_bytes=64)
             scales = work.tile([P, PASSES * NB], U8, name="scales", bufs=2, align_bytes=64)
-            nc.vector.quantize_mx(out=codes[:].bitcast(FP8X4), scales=scales[:], in_=grouped[m][:])
             x_codes[m] = codes
             x_scales[m] = scales
+            if m > 0:
+                nc.vector.quantize_mx(
+                    out=codes[:].bitcast(FP8X4), scales=scales[:], in_=grouped[m][:]
+                )
+
+        def quantise_unit(u):
+            m, r = divmod(u, SUB)
+            for c in range(PASSES):
+                c0 = c * NB + r * P
+                nc.vector.quantize_mx(
+                    out=x_codes[m][:, c0 : c0 + P].bitcast(FP8X4),
+                    scales=x_scales[m][:, c0 : c0 + P],
+                    in_=grouped[m][:, 4 * c0 : 4 * (c0 + P)],
+                )
 
         def multiply(i):
             nb, g, ob = where(i)
@@ -223,7 +239,7 @@ def tile_groupkanlayer_t_e_kernel(tc, x, W_words, W_scales, b, p, q, out):
         def product_two(i):
             nb, g, ob = where(i)
             k = g * OBS + ob
-            res = work.tile([P, 2, NB], F32, name="m2")
+            res = work.tile([P, 2, NB], F32, name="m2", bufs=4)
             nc.vector.scalar_tensor_tensor(
                 out=res[:],
                 in0=sums[i][:].unsqueeze(1).to_broadcast([P, 2, NB]),
@@ -234,14 +250,16 @@ def tile_groupkanlayer_t_e_kernel(tc, x, W_words, W_scales, b, p, q, out):
             )
             prod2[i] = res
 
-        def turn_back(i):
+        def turn_back_q(i):
             qt = psum.tile([P, SUB, P], F32, name="qt", bufs=1)
             for j in range(SUB):
                 nc.tensor.transpose(qt[:, j, :], prod2[i][:, 0, j * P : (j + 1) * P], ident[:])
+            q_back[i] = qt
+
+        def turn_back_n(i):
             nt = psum.tile([P, SUB, P], F32, name="nt")
             for j in range(SUB):
                 nc.tensor.transpose(nt[:, j, :], prod2[i][:, 1, j * P : (j + 1) * P], ident[:])
-            q_back[i] = qt
             n_back[i] = nt
 
         def magnitude(i):
@@ -258,48 +276,89 @@ def tile_groupkanlayer_t_e_kernel(tc, x, W_words, W_scales, b, p, q, out):
             )
             den[i] = d5
 
-        def inverse(i):
-            d6 = work.tile([P, NB], F32, name="d6")
-            if SQUARE_ON_GPSIMD:
+        def inverse(i, on_gpsimd):
+            if (i % OBS in SQUARE_ON_GPSIMD) != on_gpsimd:
+                return
+            d6 = work.tile([P, NB], F32, name="d6", bufs=4)
+            if on_gpsimd:
                 nc.gpsimd.tensor_tensor(out=d6[:], in0=den[i][:], in1=den[i][:], op=ALU.mult)
             else:
                 nc.scalar.activation(out=d6[:], in_=den[i][:], func=ACT.Square)
             den[i] = d6
 
-        def divide_and_store(i):
+        def inverse_s(i):
+            inverse(i, False)
+
+        def inverse_g(i):
+            inverse(i, True)
+
+        def numerator(i):
             nb, g, ob = where(i)
+            if ob in FINAL_ON_GPSIMD:
+                n1 = work.tile([P, NB], F32, name="n1")
+                nc.scalar.activation(
+                    out=n1[:], in_=n_back[i][:].rearrange("p j o -> p (j o)"), func=ACT.Identity,
+                    bias=p_coef(g, 0),
+                )
+                n_back[i] = n1
+
+        def divide_and_store(i, on_gpsimd):
+            nb, g, ob = where(i)
+            if (ob in FINAL_ON_GPSIMD) != on_gpsimd:
+                return
             res = work.tile([P, SUB, P], F32, name="res", bufs=4)
-            nc.vector.scalar_tensor_tensor(
-                out=res[:].rearrange("p j o -> p (j o)"),
-                in0=n_back[i][:].rearrange("p j o -> p (j o)"),
-                scalar=p_coef(g, 0),
-                in1=den[i][:],
-                op0=ALU.add,
-                op1=ALU.mult,
-            )
+            if on_gpsimd:
+                nc.gpsimd.tensor_tensor(
+                    out=res[:].rearrange("p j o -> p (j o)"), in0=n_back[i][:], in1=den[i][:],
+                    op=ALU.mult,
+                )
+            else:
+                nc.vector.scalar_tensor_tensor(
+                    out=res[:].rearrange("p j o -> p (j o)"),
+                    in0=n_back[i][:].rearrange("p j o -> p (j o)"),
+                    scalar=p_coef(g, 0),
+                    in1=den[i][:],
+                    op0=ALU.add,
+                    op1=ALU.mult,
+                )
             col0 = g * GOUT + ob * P
             nc.sync.dma_start(
                 out=out[nb * NB : (nb + 1) * NB, col0 : col0 + P].rearrange("(j r) o -> r j o", r=P),
                 in_=res[:],
             )
 
+        def divide_v(i):
+            divide_and_store(i, False)
+
+        def divide_g(i):
+            divide_and_store(i, True)
+
         def run(stage, i, count=TILES):
             if 0 <= i < count:
                 stage(i)
 
-        for t in range(-8, TILES + 3):
-            run(inverse, t - 2)
+        for t in range(-8, TILES + 4):
             run(square_y, t + 1)
             run(outer_terms, t + 1)
             run(quadratics, t)
-            if (t + 3) % OBS == 0:
+            if t == -8:
+                quantise_x(0)
+            elif (t + 3) % OBS == 0 and t + 3 >= OBS:
                 run(quantise_x, (t + 3) // OBS, MACROS)
-            run(divide_and_store, t - 2)
+            run(inverse_g, t - 2)
+            run(divide_g, t - 3)
+            run(divide_v, t - 3)
             run(product_two, t)
-            run(turn_back, t - 1)
+            run(turn_back_q, t - 1)
+            run(turn_back_n, t - 2)
             run(magnitude, t - 1)
             run(group_x, t + 7, UNITS)
+            run(quantise_unit, t + 7, SUB)
             run(inverse_root, t - 1)
+            run(inverse_s, t - 2)
+            run(numerator, t - 2)
             run(turn_x, t + 8, UNITS)
+            if t == -4:
+                channel_constants()
             run(multiply, t + 2)
             run(load_x, t + 8 + LOADS_AHEAD, UNITS)

@@ -29,7 +29,7 @@ TILES = MACROS * OBS
 UNITS = MACROS * SUB
 LOADS_AHEAD = 8
 SQUARE_ON_GPSIMD = ()
-FINAL_ON_GPSIMD = (3,)
+FINAL_ON_GPSIMD = (1,)
 
 FLOPS = 2 * ROWS * GROUPS * GIN * GOUT
 
@@ -213,11 +213,12 @@ def tile_groupkanlayer_t_e_kernel(tc, x, W_words, W_scales, b, p, q, out):
             nb, g, ob = where(i)
             k = g * OBS + ob
             e = work.tile([P, 2, NB], F32, name="e")
-            nc.gpsimd.tensor_scalar(
+            engine = nc.vector if i == 0 else nc.gpsimd
+            engine.tensor_scalar(
                 out=e[:, 0, :], in0=first[i][:], scalar1=q_coef(g, 3),
                 scalar2=mid_const_q[:, k : k + 1], op0=ALU.mult, op1=ALU.add,
             )
-            nc.gpsimd.tensor_scalar(
+            engine.tensor_scalar(
                 out=e[:, 1, :], in0=first[i][:], scalar1=p_coef(g, 3),
                 scalar2=mid_const_p[:, k : k + 1], op0=ALU.mult, op1=ALU.add,
             )
@@ -239,15 +240,22 @@ def tile_groupkanlayer_t_e_kernel(tc, x, W_words, W_scales, b, p, q, out):
         def product_two(i):
             nb, g, ob = where(i)
             k = g * OBS + ob
-            res = work.tile([P, 2, NB], F32, name="m2", bufs=4)
-            nc.vector.scalar_tensor_tensor(
-                out=res[:],
-                in0=sums[i][:].unsqueeze(1).to_broadcast([P, 2, NB]),
-                scalar=b_col[:, k : k + 1],
-                in1=plus1[i][:],
-                op0=ALU.add,
-                op1=ALU.mult,
-            )
+            res = work.tile([P, 2, NB], F32, name="m2", bufs=5)
+            if i == TILES - 1:
+                for slot in range(2):
+                    nc.vector.scalar_tensor_tensor(
+                        out=res[:, slot, :], in0=sums[i][:], scalar=b_col[:, k : k + 1],
+                        in1=plus1[i][:, slot, :], op0=ALU.add, op1=ALU.mult,
+                    )
+            else:
+                nc.vector.scalar_tensor_tensor(
+                    out=res[:],
+                    in0=sums[i][:].unsqueeze(1).to_broadcast([P, 2, NB]),
+                    scalar=b_col[:, k : k + 1],
+                    in1=plus1[i][:],
+                    op0=ALU.add,
+                    op1=ALU.mult,
+                )
             prod2[i] = res
 
         def turn_back_q(i):
@@ -337,26 +345,26 @@ def tile_groupkanlayer_t_e_kernel(tc, x, W_words, W_scales, b, p, q, out):
             if 0 <= i < count:
                 stage(i)
 
-        for t in range(-8, TILES + 4):
-            run(square_y, t + 1)
-            run(outer_terms, t + 1)
-            run(quadratics, t)
+        for t in range(-8, TILES + 5):
             if t == -8:
                 quantise_x(0)
             elif (t + 3) % OBS == 0 and t + 3 >= OBS:
                 run(quantise_x, (t + 3) // OBS, MACROS)
-            run(inverse_g, t - 2)
-            run(divide_g, t - 3)
-            run(divide_v, t - 3)
+            run(square_y, t + 1)
+            run(outer_terms, t + 1)
+            run(quadratics, t)
+            run(inverse_g, t - 3)
+            run(divide_g, t - 4)
+            run(divide_v, t - 4)
             run(product_two, t)
-            run(turn_back_q, t - 1)
-            run(turn_back_n, t - 2)
-            run(magnitude, t - 1)
+            run(turn_back_q, t - 2)
+            run(turn_back_n, t - 3)
+            run(magnitude, t - 2)
             run(group_x, t + 7, UNITS)
             run(quantise_unit, t + 7, SUB)
-            run(inverse_root, t - 1)
-            run(inverse_s, t - 2)
-            run(numerator, t - 2)
+            run(inverse_root, t - 2)
+            run(inverse_s, t - 3)
+            run(numerator, t - 3)
             run(turn_x, t + 8, UNITS)
             if t == -4:
                 channel_constants()

@@ -29,7 +29,7 @@ TILES = MACROS * OBS
 UNITS = MACROS * SUB
 LOADS_AHEAD = 8
 SQUARE_ON_GPSIMD = ()
-FINAL_ON_GPSIMD = (1,)
+FINAL_ON_GPSIMD = (0,)
 
 FLOPS = 2 * ROWS * GROUPS * GIN * GOUT
 
@@ -133,6 +133,7 @@ def tile_groupkanlayer_t_e_kernel(tc, x, W_words, W_scales, b, p, q, out):
         q_back = {}
         n_back = {}
         den = {}
+        results = {}
 
         def where(i):
             m, ob = divmod(i, OBS)
@@ -240,7 +241,7 @@ def tile_groupkanlayer_t_e_kernel(tc, x, W_words, W_scales, b, p, q, out):
         def product_two(i):
             nb, g, ob = where(i)
             k = g * OBS + ob
-            res = work.tile([P, 2, NB], F32, name="m2", bufs=5)
+            res = work.tile([P, 2, NB], F32, name="m2", bufs=6)
             if i == TILES - 1:
                 for slot in range(2):
                     nc.vector.scalar_tensor_tensor(
@@ -287,7 +288,7 @@ def tile_groupkanlayer_t_e_kernel(tc, x, W_words, W_scales, b, p, q, out):
         def inverse(i, on_gpsimd):
             if (i % OBS in SQUARE_ON_GPSIMD) != on_gpsimd:
                 return
-            d6 = work.tile([P, NB], F32, name="d6", bufs=4)
+            d6 = work.tile([P, NB], F32, name="d6", bufs=5)
             if on_gpsimd:
                 nc.gpsimd.tensor_tensor(out=d6[:], in0=den[i][:], in1=den[i][:], op=ALU.mult)
             else:
@@ -314,26 +315,37 @@ def tile_groupkanlayer_t_e_kernel(tc, x, W_words, W_scales, b, p, q, out):
             nb, g, ob = where(i)
             if (ob in FINAL_ON_GPSIMD) != on_gpsimd:
                 return
-            res = work.tile([P, SUB, P], F32, name="res", bufs=4)
+            m = i // OBS
+            if m not in results:
+                res_new = work.tile([P, SUB, OBS, P], F32, name="res", bufs=3)
+                results[m] = res_new
+            res = results[m]
             if on_gpsimd:
                 nc.gpsimd.tensor_tensor(
-                    out=res[:].rearrange("p j o -> p (j o)"), in0=n_back[i][:], in1=den[i][:],
+                    out=res[:, :, ob, :],
+                    in0=n_back[i][:].rearrange("p (j o) -> p j o", j=SUB),
+                    in1=den[i][:].rearrange("p (j o) -> p j o", j=SUB),
                     op=ALU.mult,
                 )
             else:
                 nc.vector.scalar_tensor_tensor(
-                    out=res[:].rearrange("p j o -> p (j o)"),
-                    in0=n_back[i][:].rearrange("p j o -> p (j o)"),
+                    out=res[:, :, ob, :],
+                    in0=n_back[i][:],
                     scalar=p_coef(g, 0),
-                    in1=den[i][:],
+                    in1=den[i][:].rearrange("p (j o) -> p j o", j=SUB),
                     op0=ALU.add,
                     op1=ALU.mult,
                 )
-            col0 = g * GOUT + ob * P
-            nc.sync.dma_start(
-                out=out[nb * NB : (nb + 1) * NB, col0 : col0 + P].rearrange("(j r) o -> r j o", r=P),
-                in_=res[:],
+            rows = out[nb * NB : (nb + 1) * NB, g * GOUT : (g + 1) * GOUT].rearrange(
+                "(j r) (k o) -> r j k o", r=P, o=P
             )
+            if m == MACROS - 1:
+                nc.sync.dma_start(out=rows[:, :, ob, :], in_=res[:, :, ob, :])
+            elif ob == OBS - 1:
+                nc.sync.dma_start(
+                    out=rows.rearrange("r j k o -> r j (k o)"),
+                    in_=res[:].rearrange("p j k o -> p j (k o)"),
+                )
 
         def divide_v(i):
             divide_and_store(i, False)
@@ -345,7 +357,7 @@ def tile_groupkanlayer_t_e_kernel(tc, x, W_words, W_scales, b, p, q, out):
             if 0 <= i < count:
                 stage(i)
 
-        for t in range(-8, TILES + 5):
+        for t in range(-8, TILES + 6):
             if t == -8:
                 quantise_x(0)
             elif (t + 3) % OBS == 0 and t + 3 >= OBS:
@@ -354,17 +366,17 @@ def tile_groupkanlayer_t_e_kernel(tc, x, W_words, W_scales, b, p, q, out):
             run(outer_terms, t + 1)
             run(quadratics, t)
             run(inverse_g, t - 3)
-            run(divide_g, t - 4)
-            run(divide_v, t - 4)
+            run(divide_g, t - 5)
+            run(divide_v, t - 5)
             run(product_two, t)
             run(turn_back_q, t - 2)
-            run(turn_back_n, t - 3)
+            run(turn_back_n, t - 4)
             run(magnitude, t - 2)
             run(group_x, t + 7, UNITS)
             run(quantise_unit, t + 7, SUB)
             run(inverse_root, t - 2)
             run(inverse_s, t - 3)
-            run(numerator, t - 3)
+            run(numerator, t - 4)
             run(turn_x, t + 8, UNITS)
             if t == -4:
                 channel_constants()

@@ -28,6 +28,7 @@ MACROS = (ROWS // NB) * GROUPS
 TILES = MACROS * OBS
 UNITS = MACROS * SUB
 LOADS_AHEAD = 8
+WARM_UP = 3
 SQUARE_ON_GPSIMD = ()
 FINAL_ON_GPSIMD = (0,)
 
@@ -52,6 +53,17 @@ def tile_groupkanlayer_t_e_kernel(tc, x, W_words, W_scales, b, p, q, out):
             nc.sync.dma_start(out=x_sb[:], in_=x[row0 : row0 + P, g * GIN : (g + 1) * GIN])
             x_part[u] = x_sb
 
+        zeros = const.tile([P, NB], BF16)
+        nc.vector.memset(zeros[:], 0.0)
+        idle = psum.tile([P, NB], F32, name="acc", bufs=3)
+        for k in range(WARM_UP):
+            nc.tensor.matmul(idle[:], lhsT=zeros[:, 0:P], rhs=zeros[:], start=True, stop=True)
+
+        one = const.tile([P, 1], F32)
+        nc.vector.memset(one[:], 1.0)
+        first_call = const.tile([P, 1], F32)
+        nc.scalar.activation(out=first_call[:], in_=one[:], func=ACT.Abs_reciprocal_sqrt)
+
         b_rows_bf = const.tile([P, P], BF16)
         nc.vector.memset(b_rows_bf[:], 0.0)
         nc.scalar.dma_start(
@@ -66,10 +78,6 @@ def tile_groupkanlayer_t_e_kernel(tc, x, W_words, W_scales, b, p, q, out):
             load_x(u)
 
         w_words = const.tile([P, GROUPS * PASSES, 2 * GOUT], U8, align_bytes=64)
-        nc.sync.dma_start(
-            out=w_words[:].bitcast(I32),
-            in_=W_words.bitcast(I32).rearrange("c p n -> p c n"),
-        )
         w_planes = const.tile([P, GROUPS * PASSES, GOUT], U8, align_bytes=64)
         nc.vector.memset(w_planes[:].bitcast(I32), 0)
         for quadrant in range(4):
@@ -79,6 +87,14 @@ def tile_groupkanlayer_t_e_kernel(tc, x, W_words, W_scales, b, p, q, out):
                     "c r n -> r c n"
                 ),
             )
+
+        def load_w(g):
+            nc.sync.dma_start(
+                out=w_words[:, g * PASSES : (g + 1) * PASSES, :].bitcast(I32),
+                in_=W_words.bitcast(I32)[g * PASSES : (g + 1) * PASSES].rearrange("c p n -> p c n"),
+            )
+
+        load_w(0)
 
         ident = const.tile([P, P], F32)
         make_identity(nc, ident[:])
@@ -97,8 +113,6 @@ def tile_groupkanlayer_t_e_kernel(tc, x, W_words, W_scales, b, p, q, out):
         def q_coef(g, power):
             return q_f32[:, 3 * g + power - 1 : 3 * g + power]
 
-        one = const.tile([P, 1], F32)
-        nc.vector.memset(one[:], 1.0)
 
         mid_const_p = const.tile([P, GROUPS * OBS], F32)
         mid_const_q = const.tile([P, GROUPS * OBS], F32)
@@ -120,6 +134,7 @@ def tile_groupkanlayer_t_e_kernel(tc, x, W_words, W_scales, b, p, q, out):
 
         for u in range(4, LOADS_AHEAD):
             load_x(u)
+        load_w(1)
 
         turned = {}
         grouped = {}
@@ -133,6 +148,8 @@ def tile_groupkanlayer_t_e_kernel(tc, x, W_words, W_scales, b, p, q, out):
         q_back = {}
         n_back = {}
         den = {}
+        pair_abs = {}
+        pair_root = {}
         results = {}
 
         def where(i):
@@ -272,38 +289,35 @@ def tile_groupkanlayer_t_e_kernel(tc, x, W_words, W_scales, b, p, q, out):
             n_back[i] = nt
 
         def magnitude(i):
-            d4 = work.tile([P, NB], F32, name="d4")
+            k, half = divmod(i, 2)
+            if half == 0:
+                d4_new = work.tile([P, 2, NB], F32, name="d4")
+                pair_abs[k] = d4_new
             nc.scalar.activation(
-                out=d4[:], in_=q_back[i][:].rearrange("p j o -> p (j o)"), func=ACT.Abs
+                out=pair_abs[k][:, half, :], in_=q_back[i][:].rearrange("p j o -> p (j o)"),
+                func=ACT.Abs,
             )
-            den[i] = d4
 
-        def inverse_root(i):
-            d5 = work.tile([P, NB], F32, name="d5")
+        def inverse_root(k):
+            d5 = work.tile([P, 2, NB], F32, name="d5")
             nc.scalar.activation(
-                out=d5[:], in_=den[i][:], func=ACT.Abs_reciprocal_sqrt, bias=one[:]
+                out=d5[:], in_=pair_abs[k][:], func=ACT.Abs_reciprocal_sqrt, bias=one[:]
             )
-            den[i] = d5
+            pair_root[k] = d5
 
-        def inverse(i, on_gpsimd):
-            if (i % OBS in SQUARE_ON_GPSIMD) != on_gpsimd:
-                return
-            d6 = work.tile([P, NB], F32, name="d6", bufs=5)
-            if on_gpsimd:
-                nc.gpsimd.tensor_tensor(out=d6[:], in0=den[i][:], in1=den[i][:], op=ALU.mult)
-            else:
-                nc.scalar.activation(out=d6[:], in_=den[i][:], func=ACT.Square)
-            den[i] = d6
+        def inverse(k):
+            d6 = work.tile([P, 2, NB], F32, name="d6")
+            nc.scalar.activation(out=d6[:], in_=pair_root[k][:], func=ACT.Square)
+            den[2 * k] = d6[:, 0, :]
+            den[2 * k + 1] = d6[:, 1, :]
 
-        def inverse_s(i):
-            inverse(i, False)
-
-        def inverse_g(i):
-            inverse(i, True)
+        def final_on_gpsimd(i):
+            m, ob = divmod(i, OBS)
+            return ob == 0 or (ob == 2 and m % 2 == 0)
 
         def numerator(i):
             nb, g, ob = where(i)
-            if ob in FINAL_ON_GPSIMD:
+            if final_on_gpsimd(i):
                 n1 = work.tile([P, NB], F32, name="n1")
                 nc.scalar.activation(
                     out=n1[:], in_=n_back[i][:].rearrange("p j o -> p (j o)"), func=ACT.Identity,
@@ -313,7 +327,7 @@ def tile_groupkanlayer_t_e_kernel(tc, x, W_words, W_scales, b, p, q, out):
 
         def divide_and_store(i, on_gpsimd):
             nb, g, ob = where(i)
-            if (ob in FINAL_ON_GPSIMD) != on_gpsimd:
+            if final_on_gpsimd(i) != on_gpsimd:
                 return
             m = i // OBS
             if m not in results:
@@ -324,7 +338,7 @@ def tile_groupkanlayer_t_e_kernel(tc, x, W_words, W_scales, b, p, q, out):
                 nc.gpsimd.tensor_tensor(
                     out=res[:, :, ob, :],
                     in0=n_back[i][:].rearrange("p (j o) -> p j o", j=SUB),
-                    in1=den[i][:].rearrange("p (j o) -> p j o", j=SUB),
+                    in1=den[i].rearrange("p (j o) -> p j o", j=SUB),
                     op=ALU.mult,
                 )
             else:
@@ -332,7 +346,7 @@ def tile_groupkanlayer_t_e_kernel(tc, x, W_words, W_scales, b, p, q, out):
                     out=res[:, :, ob, :],
                     in0=n_back[i][:],
                     scalar=p_coef(g, 0),
-                    in1=den[i][:].rearrange("p (j o) -> p j o", j=SUB),
+                    in1=den[i].rearrange("p (j o) -> p j o", j=SUB),
                     op0=ALU.add,
                     op1=ALU.mult,
                 )
@@ -353,6 +367,13 @@ def tile_groupkanlayer_t_e_kernel(tc, x, W_words, W_scales, b, p, q, out):
         def divide_g(i):
             divide_and_store(i, True)
 
+        def units_turned_at(t):
+            if t in (-2, -1):
+                return [2 * t + 8, 2 * t + 9]
+            if -4 <= t < 0 or not 0 <= t + 8 < UNITS:
+                return []
+            return [t + 8]
+
         def run(stage, i, count=TILES):
             if 0 <= i < count:
                 stage(i)
@@ -365,20 +386,27 @@ def tile_groupkanlayer_t_e_kernel(tc, x, W_words, W_scales, b, p, q, out):
             run(square_y, t + 1)
             run(outer_terms, t + 1)
             run(quadratics, t)
-            run(inverse_g, t - 3)
             run(divide_g, t - 5)
             run(divide_v, t - 5)
             run(product_two, t)
             run(turn_back_q, t - 2)
             run(turn_back_n, t - 4)
             run(magnitude, t - 2)
-            run(group_x, t + 7, UNITS)
-            run(quantise_unit, t + 7, SUB)
-            run(inverse_root, t - 2)
-            run(inverse_s, t - 3)
+            for u in units_turned_at(t - 1):
+                group_x(u)
+                if u < SUB:
+                    quantise_unit(u)
+            if t % 2 == 1:
+                run(inverse_root, (t - 3) // 2, TILES // 2)
+            else:
+                run(inverse, (t - 4) // 2, TILES // 2)
             run(numerator, t - 4)
-            run(turn_x, t + 8, UNITS)
-            if t == -4:
+            if t < 0:
+                run(multiply, t + 2)
+            for u in units_turned_at(t):
+                turn_x(u)
+            if t == -5:
                 channel_constants()
-            run(multiply, t + 2)
+            if t >= 0:
+                run(multiply, t + 2)
             run(load_x, t + 8 + LOADS_AHEAD, UNITS)

@@ -69,10 +69,12 @@ def tile_groupkanlayer_t_e_kernel(tc, x, W_words, W_scales, b, p, q, out):
         nc.scalar.dma_start(
             out=b_rows_bf[0 : GROUPS * OBS, :], in_=b.rearrange("g (k c) -> (g k) c", c=P)
         )
-        p_bf = const.tile([P, GROUPS * 4], BF16)
-        nc.scalar.dma_start(out=p_bf[:], in_=p.rearrange("g c -> (g c)").partition_broadcast(P))
-        q_bf = const.tile([P, GROUPS * 3], BF16)
-        nc.scalar.dma_start(out=q_bf[:], in_=q.rearrange("g c -> (g c)").partition_broadcast(P))
+        pq_row = const.tile([P, 32], BF16)
+        nc.vector.memset(pq_row[:], 0.0)
+        nc.scalar.dma_start(out=pq_row[0:1, 0:8], in_=p.rearrange("(a g) c -> a (g c)", a=1))
+        nc.scalar.dma_start(out=pq_row[0:1, 16:22], in_=q.rearrange("(a g) c -> a (g c)", a=1))
+        ones_bf = const.tile([P, P], BF16)
+        nc.vector.memset(ones_bf[:], 1.0)
 
         for u in range(4):
             load_x(u)
@@ -102,22 +104,22 @@ def tile_groupkanlayer_t_e_kernel(tc, x, W_words, W_scales, b, p, q, out):
         b_rows = const.tile([P, P], F32)
         nc.vector.tensor_copy(out=b_rows[:], in_=b_rows_bf[:])
         b_col = const.tile([P, GROUPS * OBS], F32)
-        p_f32 = const.tile([P, GROUPS * 4], F32)
-        nc.vector.tensor_copy(out=p_f32[:], in_=p_bf[:])
-        q_f32 = const.tile([P, GROUPS * 3], F32)
-        nc.vector.tensor_copy(out=q_f32[:], in_=q_bf[:])
+        pq_f32 = const.tile([P, 32], F32)
 
         def p_coef(g, power):
-            return p_f32[:, 4 * g + power : 4 * g + power + 1]
+            return pq_f32[:, 4 * g + power : 4 * g + power + 1]
 
         def q_coef(g, power):
-            return q_f32[:, 3 * g + power - 1 : 3 * g + power]
+            return pq_f32[:, 16 + 3 * g + power - 1 : 16 + 3 * g + power]
 
 
         mid_const_p = const.tile([P, GROUPS * OBS], F32)
         mid_const_q = const.tile([P, GROUPS * OBS], F32)
 
         def channel_constants():
+            pq_all = psum.tile([P, SUB, P], F32, name="qt", bufs=1)
+            nc.tensor.matmul(pq_all[:, 0, 0:32], lhsT=ones_bf[:], rhs=pq_row[:], start=True, stop=True)
+            nc.vector.tensor_copy(out=pq_f32[:], in_=pq_all[:, 0, 0:32])
             b_turned = psum.tile([P, SUB, P], F32, name="nt")
             nc.tensor.transpose(b_turned[:, 0, :], b_rows[:], ident[:])
             nc.vector.tensor_copy(out=b_col[:], in_=b_turned[:, 0, 0 : GROUPS * OBS])
@@ -150,6 +152,7 @@ def tile_groupkanlayer_t_e_kernel(tc, x, W_words, W_scales, b, p, q, out):
         den = {}
         pair_abs = {}
         pair_root = {}
+        pair_inv = {}
         results = {}
 
         def where(i):
@@ -305,6 +308,26 @@ def tile_groupkanlayer_t_e_kernel(tc, x, W_words, W_scales, b, p, q, out):
             )
             pair_root[k] = d5
 
+        def inverse_root_last(i):
+            k, half = divmod(i, 2)
+            if half == 0:
+                d5_new = work.tile([P, 2, NB], F32, name="d5")
+                pair_root[k] = d5_new
+            nc.scalar.activation(
+                out=pair_root[k][:, half, :], in_=pair_abs[k][:, half, :],
+                func=ACT.Abs_reciprocal_sqrt, bias=one[:],
+            )
+
+        def inverse_last(i):
+            k, half = divmod(i, 2)
+            if half == 0:
+                d6_new = work.tile([P, 2, NB], F32, name="d6")
+                pair_inv[k] = d6_new
+            nc.scalar.activation(
+                out=pair_inv[k][:, half, :], in_=pair_root[k][:, half, :], func=ACT.Square
+            )
+            den[i] = pair_inv[k][:, half, :]
+
         def inverse(k):
             d6 = work.tile([P, 2, NB], F32, name="d6")
             nc.scalar.activation(out=d6[:], in_=pair_root[k][:], func=ACT.Square)
@@ -397,9 +420,13 @@ def tile_groupkanlayer_t_e_kernel(tc, x, W_words, W_scales, b, p, q, out):
                 if u < SUB:
                     quantise_unit(u)
             if t % 2 == 1:
-                run(inverse_root, (t - 3) // 2, TILES // 2)
+                run(inverse_root, (t - 3) // 2, TILES // 2 - 1)
             else:
-                run(inverse, (t - 4) // 2, TILES // 2)
+                run(inverse, (t - 4) // 2, TILES // 2 - 1)
+            if t - 2 >= TILES - 2:
+                run(inverse_root_last, t - 2)
+            if t - 3 >= TILES - 2:
+                run(inverse_last, t - 3)
             run(numerator, t - 4)
             if t < 0:
                 run(multiply, t + 2)

@@ -113,9 +113,6 @@ def tile_groupkanlayer_t_e_kernel(tc, x, W_words, W_scales, b, p, q, out):
             return pq_f32[:, 16 + 3 * g + power - 1 : 16 + 3 * g + power]
 
 
-        mid_const_p = const.tile([P, GROUPS * OBS], F32)
-        mid_const_q = const.tile([P, GROUPS * OBS], F32)
-
         def channel_constants():
             pq_all = psum.tile([P, SUB, P], F32, name="qt", bufs=1)
             nc.tensor.matmul(pq_all[:, 0, 0:32], lhsT=ones_bf[:], rhs=pq_row[:], start=True, stop=True)
@@ -123,16 +120,6 @@ def tile_groupkanlayer_t_e_kernel(tc, x, W_words, W_scales, b, p, q, out):
             b_turned = psum.tile([P, SUB, P], F32, name="nt")
             nc.tensor.transpose(b_turned[:, 0, :], b_rows[:], ident[:])
             nc.vector.tensor_copy(out=b_col[:], in_=b_turned[:, 0, 0 : GROUPS * OBS])
-            for g in range(GROUPS):
-                cols = slice(g * OBS, (g + 1) * OBS)
-                nc.vector.tensor_scalar(
-                    out=mid_const_p[:, cols], in0=b_col[:, cols], scalar1=p_coef(g, 2),
-                    scalar2=p_coef(g, 1), op0=ALU.mult, op1=ALU.add,
-                )
-                nc.vector.tensor_scalar(
-                    out=mid_const_q[:, cols], in0=b_col[:, cols], scalar1=q_coef(g, 2),
-                    scalar2=q_coef(g, 1), op0=ALU.mult, op1=ALU.add,
-                )
 
         for u in range(4, LOADS_AHEAD):
             load_x(u)
@@ -232,36 +219,32 @@ def tile_groupkanlayer_t_e_kernel(tc, x, W_words, W_scales, b, p, q, out):
 
         def outer_terms(i):
             nb, g, ob = where(i)
-            k = g * OBS + ob
-            e = work.tile([P, 2, NB], F32, name="e")
+            h = work.tile([P, 2, NB], F32, name="h1")
             engine = nc.vector if i == 0 else nc.gpsimd
             engine.tensor_scalar(
-                out=e[:, 0, :], in0=first[i][:], scalar1=q_coef(g, 3),
-                scalar2=mid_const_q[:, k : k + 1], op0=ALU.mult, op1=ALU.add,
+                out=h[:, 0, :], in0=first[i][:], scalar1=q_coef(g, 3),
+                scalar2=q_coef(g, 1), op0=ALU.mult, op1=ALU.add,
             )
             engine.tensor_scalar(
-                out=e[:, 1, :], in0=first[i][:], scalar1=p_coef(g, 3),
-                scalar2=mid_const_p[:, k : k + 1], op0=ALU.mult, op1=ALU.add,
+                out=h[:, 1, :], in0=first[i][:], scalar1=p_coef(g, 3),
+                scalar2=p_coef(g, 1), op0=ALU.mult, op1=ALU.add,
             )
-            prod1[i] = e
+            plus1[i] = h
 
         def quadratics(i):
             nb, g, ob = where(i)
-            h = work.tile([P, 2, NB], F32, name="h1")
-            nc.vector.scalar_tensor_tensor(
-                out=h[:, 0, :], in0=sums[i][:], scalar=q_coef(g, 2), in1=prod1[i][:, 0, :],
-                op0=ALU.mult, op1=ALU.add,
+            res = work.tile([P, 4, NB], F32, name="m2", bufs=6)
+            nc.vector.tensor_scalar_mul(out=res[:, 2, :], in0=first[i][:], scalar1=q_coef(g, 2))
+            nc.vector.tensor_scalar(
+                out=res[:, 3, :], in0=first[i][:], scalar1=p_coef(g, 2),
+                scalar2=p_coef(g, 0), op0=ALU.mult, op1=ALU.add,
             )
-            nc.vector.scalar_tensor_tensor(
-                out=h[:, 1, :], in0=sums[i][:], scalar=p_coef(g, 2), in1=prod1[i][:, 1, :],
-                op0=ALU.mult, op1=ALU.add,
-            )
-            plus1[i] = h
+            prod2[i] = res
 
         def product_two(i):
             nb, g, ob = where(i)
             k = g * OBS + ob
-            res = work.tile([P, 2, NB], F32, name="m2", bufs=6)
+            res = prod2[i]
             if i == TILES - 1:
                 for slot in range(2):
                     nc.vector.scalar_tensor_tensor(
@@ -270,25 +253,32 @@ def tile_groupkanlayer_t_e_kernel(tc, x, W_words, W_scales, b, p, q, out):
                     )
             else:
                 nc.vector.scalar_tensor_tensor(
-                    out=res[:],
+                    out=res[:, 0:2, :],
                     in0=sums[i][:].unsqueeze(1).to_broadcast([P, 2, NB]),
                     scalar=b_col[:, k : k + 1],
                     in1=plus1[i][:],
                     op0=ALU.add,
                     op1=ALU.mult,
                 )
-            prod2[i] = res
 
         def turn_back_q(i):
             qt = psum.tile([P, SUB, P], F32, name="qt", bufs=1)
             for j in range(SUB):
-                nc.tensor.transpose(qt[:, j, :], prod2[i][:, 0, j * P : (j + 1) * P], ident[:])
+                for slot in (0, 2):
+                    nc.tensor.matmul(
+                        qt[:, j, :], lhsT=prod2[i][:, slot, j * P : (j + 1) * P], rhs=ident[:],
+                        is_transpose=True, start=(slot == 0), stop=(slot == 2),
+                    )
             q_back[i] = qt
 
         def turn_back_n(i):
             nt = psum.tile([P, SUB, P], F32, name="nt")
             for j in range(SUB):
-                nc.tensor.transpose(nt[:, j, :], prod2[i][:, 1, j * P : (j + 1) * P], ident[:])
+                for slot in (1, 3):
+                    nc.tensor.matmul(
+                        nt[:, j, :], lhsT=prod2[i][:, slot, j * P : (j + 1) * P], rhs=ident[:],
+                        is_transpose=True, start=(slot == 1), stop=(slot == 3),
+                    )
             n_back[i] = nt
 
         def magnitude(i):
@@ -335,17 +325,13 @@ def tile_groupkanlayer_t_e_kernel(tc, x, W_words, W_scales, b, p, q, out):
             den[2 * k + 1] = d6[:, 1, :]
 
         def final_on_gpsimd(i):
-            m, ob = divmod(i, OBS)
-            return ob == 0 or (ob == 2 and m % 2 == 0)
+            return False
 
         def numerator(i):
             nb, g, ob = where(i)
             if final_on_gpsimd(i):
                 n1 = work.tile([P, NB], F32, name="n1")
-                nc.scalar.activation(
-                    out=n1[:], in_=n_back[i][:].rearrange("p j o -> p (j o)"), func=ACT.Identity,
-                    bias=p_coef(g, 0),
-                )
+                nc.scalar.copy(out=n1[:], in_=n_back[i][:].rearrange("p j o -> p (j o)"))
                 n_back[i] = n1
 
         def divide_and_store(i, on_gpsimd):
@@ -365,13 +351,11 @@ def tile_groupkanlayer_t_e_kernel(tc, x, W_words, W_scales, b, p, q, out):
                     op=ALU.mult,
                 )
             else:
-                nc.vector.scalar_tensor_tensor(
+                nc.vector.tensor_tensor(
                     out=res[:, :, ob, :],
                     in0=n_back[i][:],
-                    scalar=p_coef(g, 0),
                     in1=den[i].rearrange("p (j o) -> p j o", j=SUB),
-                    op0=ALU.add,
-                    op1=ALU.mult,
+                    op=ALU.mult,
                 )
             rows = out[nb * NB : (nb + 1) * NB, g * GOUT : (g + 1) * GOUT].rearrange(
                 "(j r) (k o) -> r j k o", r=P, o=P

@@ -164,7 +164,8 @@ def tile_groupkanlayer_t_e_kernel(tc, x, W_words, W_scales, b, p, q, out):
                 gx_new = work.tile([P, PASSES * NB * 4], BF16, name="gx", bufs=2, align_bytes=64)
                 grouped[m] = gx_new
             gx = grouped[m]
-            nc.scalar.copy(
+            copy = nc.vector.tensor_copy if (r == 2 and m >= 2) else nc.scalar.copy
+            copy(
                 out=gx[:].bitcast(F32).rearrange("p (c n h) -> p c n h", c=PASSES, h=2)[
                     :, :, r * P : (r + 1) * P, :
                 ],

from contextlib import ExitStack

import concourse.mybir as mybir
from concourse.masks import make_identity

F32 = mybir.dt.float32
BF16 = mybir.dt.bfloat16
I32 = mybir.dt.int32
U32 = mybir.dt.uint32
U8 = mybir.dt.uint8
FP8X4 = mybir.dt.float8_e4m3fn_x4
FP4X4 = mybir.dt.float4_e2m1fn_x4
ALU = mybir.AluOpType
ACT = mybir.ActivationFunctionType

P = 128
ROWS = 4096
GROUPS = 2
GIN = 1024
GOUT = 512
K_PASS = 512
PASSES = GIN // K_PASS
WORDS_PASS = K_PASS // 2
NB = 512
SUB = NB // P
OBS = GOUT // P
MACROS = (ROWS // NB) * GROUPS
TILES = MACROS * OBS
UNITS = MACROS * SUB
LOADS_AHEAD = 8
WARM_UP = 3
SQUARE_ON_GPSIMD = ()
FINAL_ON_GPSIMD = (0,)

FLOPS = 2 * ROWS * GROUPS * GIN * GOUT


def tile_groupkanlayer_t_e_kernel(tc, x, W_words, W_scales, b, p, q, out):
    nc = tc.nc
    with ExitStack() as stack:
        stack.enter_context(tc.manual_schedule())
        const = stack.enter_context(tc.tile_pool(name="const", bufs=1))
        work = stack.enter_context(tc.tile_pool(name="work", bufs=3))
        psum = stack.enter_context(tc.psum_pool(name="psum", bufs=2))

        x_part = {}

        def load_x(u):
            m, r = divmod(u, SUB)
            nb, g = divmod(m, GROUPS)
            x_sb = work.tile([P, GIN], BF16, name="x_sb", bufs=LOADS_AHEAD + 2)
            row0 = nb * NB + r * P
            nc.sync.dma_start(out=x_sb[:], in_=x[row0 : row0 + P, g * GIN : (g + 1) * GIN])
            x_part[u] = x_sb

        zeros = const.tile([P, NB], BF16)
        nc.vector.memset(zeros[:], 0.0)
        idle = psum.tile([P, NB], F32, name="acc", bufs=3)
        for k in range(WARM_UP):
            nc.tensor.matmul(idle[:], lhsT=zeros[:, 0:P], rhs=zeros[:], start=True, stop=True)

        one = const.tile([P, 1], F32)
        nc.vector.memset(one[:], 1.0)
        first_call = const.tile([P, 1], F32)
        nc.scalar.activation(out=first_call[:], in_=one[:], func=ACT.Abs_reciprocal_sqrt)

        b_rows_bf = const.tile([P, P], BF16)
        nc.vector.memset(b_rows_bf[:], 0.0)
        nc.scalar.dma_start(
            out=b_rows_bf[0 : GROUPS * OBS, :], in_=b.rearrange("g (k c) -> (g k) c", c=P)
        )
        pq_row = const.tile([P, 32], BF16)
        nc.vector.memset(pq_row[:], 0.0)
        nc.scalar.dma_start(out=pq_row[0:1, 0:8], in_=p.rearrange("(a g) c -> a (g c)", a=1))
        nc.scalar.dma_start(out=pq_row[0:1, 16:22], in_=q.rearrange("(a g) c -> a (g c)", a=1))
        ones_bf = const.tile([P, P], BF16)
        nc.vector.memset(ones_bf[:], 1.0)

        for u in range(4):
            load_x(u)

        w_words = const.tile([P, GROUPS * PASSES, 2 * GOUT], U8, align_bytes=64)
        w_planes = const.tile([P, GROUPS * PASSES, GOUT], U8, align_bytes=64)
        nc.vector.memset(w_planes[:].bitcast(I32), 0)
        for quadrant in range(4):
            nc.sync.dma_start(
                out=w_planes[32 * quadrant : 32 * quadrant + 4].bitcast(I32),
                in_=W_scales.bitcast(I32)[:, 4 * quadrant : 4 * quadrant + 4, :].rearrange(
                    "c r n -> r c n"
                ),
            )

        def load_w(g):
            nc.sync.dma_start(
                out=w_words[:, g * PASSES : (g + 1) * PASSES, :].bitcast(I32),
                in_=W_words.bitcast(I32)[g * PASSES : (g + 1) * PASSES].rearrange("c p n -> p c n"),
            )

        load_w(0)

        ident = const.tile([P, P], F32)
        make_identity(nc, ident[:])

        b_rows = const.tile([P, P], F32)
        nc.vector.tensor_copy(out=b_rows[:], in_=b_rows_bf[:])
        b_col = const.tile([P, GROUPS * OBS], F32)
        pq_f32 = const.tile([P, 32], F32)

        def p_coef(g, power):
            return pq_f32[:, 4 * g + power : 4 * g + power + 1]

        def q_coef(g, power):
            return pq_f32[:, 16 + 3 * g + power - 1 : 16 + 3 * g + power]


        def channel_constants():
            pq_all = psum.tile([P, SUB, P], F32, name="qt", bufs=1)
            nc.tensor.matmul(pq_all[:, 0, 0:32], lhsT=ones_bf[:], rhs=pq_row[:], start=True, stop=True)
            nc.vector.tensor_copy(out=pq_f32[:], in_=pq_all[:, 0, 0:32])
            b_turned = psum.tile([P, SUB, P], F32, name="nt")
            nc.tensor.transpose(b_turned[:, 0, :], b_rows[:], ident[:])
            nc.vector.tensor_copy(out=b_col[:], in_=b_turned[:, 0, 0 : GROUPS * OBS])

        for u in range(4, LOADS_AHEAD):
            load_x(u)
        load_w(1)

        turned = {}
        grouped = {}
        x_codes = {}
        x_scales = {}
        sums = {}
        first = {}
        prod1 = {}
        plus1 = {}
        prod2 = {}
        q_back = {}
        n_back = {}
        den = {}
        pair_abs = {}
        pair_root = {}
        pair_inv = {}
        results = {}

        def where(i):
            m, ob = divmod(i, OBS)
            nb, g = divmod(m, GROUPS)
            return nb, g, ob

        def turn_x(u):
            x_words = x_part[u][:].bitcast(F32)
            xt = psum.tile([P, PASSES, 2, P], F32, name="xt")
            for c in range(PASSES):
                w0 = c * WORDS_PASS
                for h in range(2):
                    nc.tensor.transpose(
                        xt[:, c, h, :], x_words[:, w0 + h : w0 + WORDS_PASS : 2], ident[:]
                    )
            turned[u] = xt

        def group_x(u):
            m, r = divmod(u, SUB)
            if r == 0:
                gx_new = work.tile([P, PASSES * NB * 4], BF16, name="gx", bufs=2, align_bytes=64)
                grouped[m] = gx_new
            gx = grouped[m]
            copy = nc.vector.tensor_copy if (r == 2 and m >= 2) else nc.scalar.copy
            copy(
                out=gx[:].bitcast(F32).rearrange("p (c n h) -> p c n h", c=PASSES, h=2)[
                    :, :, r * P : (r + 1) * P, :
                ],
                in_=turned[u][:].rearrange("p c h n -> p c n h"),
            )

        def quantise_x(m):
            codes = work.tile([P, PASSES * NB], U32, name="codes", bufs=2, align_bytes=64)
            scales = work.tile([P, PASSES * NB], U8, name="scales", bufs=2, align_bytes=64)
            x_codes[m] = codes
            x_scales[m] = scales
            if m > 0:
                nc.vector.quantize_mx(
                    out=codes[:].bitcast(FP8X4), scales=scales[:], in_=grouped[m][:]
                )

        def quantise_unit(u):
            m, r = divmod(u, SUB)
            for c in range(PASSES):
                c0 = c * NB + r * P
                nc.vector.quantize_mx(
                    out=x_codes[m][:, c0 : c0 + P].bitcast(FP8X4),
                    scales=x_scales[m][:, c0 : c0 + P],
                    in_=grouped[m][:, 4 * c0 : 4 * (c0 + P)],
                )

        def multiply(i):
            nb, g, ob = where(i)
            m = i // OBS
            acc = psum.tile([P, NB], F32, name="acc", bufs=3)
            for c in range(PASSES):
                cols = slice(c * NB, (c + 1) * NB)
                nc.tensor.matmul_mx(
                    out=acc[:],
                    lhsT=w_words[:, g * PASSES + c, ob * 2 * P : (ob + 1) * 2 * P].bitcast(FP4X4),
                    lhsT_scale=w_planes[:, g * PASSES + c, ob * P : (ob + 1) * P],
                    rhs=x_codes[m][:, cols].bitcast(FP8X4),
                    rhs_scale=x_scales[m][:, cols],
                    start=(c == 0),
                    stop=(c == PASSES - 1),
                )
            sums[i] = acc

        def square_y(i):
            nb, g, ob = where(i)
            k = g * OBS + ob
            y2 = work.tile([P, NB], F32, name="y2")
            nc.scalar.activation(
                out=y2[:], in_=sums[i][:], func=ACT.Square, bias=b_col[:, k : k + 1]
            )
            first[i] = y2

        def outer_terms(i):
            nb, g, ob = where(i)
            h = work.tile([P, 2, NB], F32, name="h1")
            engine = nc.vector if i == 0 else nc.gpsimd
            engine.tensor_scalar(
                out=h[:, 0, :], in0=first[i][:], scalar1=q_coef(g, 3),
                scalar2=q_coef(g, 1), op0=ALU.mult, op1=ALU.add,
            )
            engine.tensor_scalar(
                out=h[:, 1, :], in0=first[i][:], scalar1=p_coef(g, 3),
                scalar2=p_coef(g, 1), op0=ALU.mult, op1=ALU.add,
            )
            plus1[i] = h

        def quadratics(i):
            nb, g, ob = where(i)
            res = work.tile([P, 4, NB], F32, name="m2", bufs=6)
            nc.vector.tensor_scalar_mul(out=res[:, 2, :], in0=first[i][:], scalar1=q_coef(g, 2))
            nc.vector.tensor_scalar(
                out=res[:, 3, :], in0=first[i][:], scalar1=p_coef(g, 2),
                scalar2=p_coef(g, 0), op0=ALU.mult, op1=ALU.add,
            )
            prod2[i] = res

        def product_two(i):
            nb, g, ob = where(i)
            k = g * OBS + ob
            res = prod2[i]
            if i == TILES - 1:
                for slot in range(2):
                    nc.vector.scalar_tensor_tensor(
                        out=res[:, slot, :], in0=sums[i][:], scalar=b_col[:, k : k + 1],
                        in1=plus1[i][:, slot, :], op0=ALU.add, op1=ALU.mult,
                    )
            else:
                nc.vector.scalar_tensor_tensor(
                    out=res[:, 0:2, :],
                    in0=sums[i][:].unsqueeze(1).to_broadcast([P, 2, NB]),
                    scalar=b_col[:, k : k + 1],
                    in1=plus1[i][:],
                    op0=ALU.add,
                    op1=ALU.mult,
                )

        def turn_back_q(i):
            qt = psum.tile([P, SUB, P], F32, name="qt", bufs=1)
            for j in range(SUB):
                for slot in (0, 2):
                    nc.tensor.matmul(
                        qt[:, j, :], lhsT=prod2[i][:, slot, j * P : (j + 1) * P], rhs=ident[:],
                        is_transpose=True, start=(slot == 0), stop=(slot == 2),
                    )
            q_back[i] = qt

        def turn_back_n(i):
            nt = psum.tile([P, SUB, P], F32, name="nt")
            for j in range(SUB):
                for slot in (1, 3):
                    nc.tensor.matmul(
                        nt[:, j, :], lhsT=prod2[i][:, slot, j * P : (j + 1) * P], rhs=ident[:],
                        is_transpose=True, start=(slot == 1), stop=(slot == 3),
                    )
            n_back[i] = nt

        def magnitude(i):
            k, half = divmod(i, 2)
            if half == 0:
                d4_new = work.tile([P, 2, NB], F32, name="d4")
                pair_abs[k] = d4_new
            nc.scalar.activation(
                out=pair_abs[k][:, half, :], in_=q_back[i][:].rearrange("p j o -> p (j o)"),
                func=ACT.Abs,
            )

        def inverse_root(k):
            d5 = work.tile([P, 2, NB], F32, name="d5")
            nc.scalar.activation(
                out=d5[:], in_=pair_abs[k][:], func=ACT.Abs_reciprocal_sqrt, bias=one[:]
            )
            pair_root[k] = d5

        def inverse_root_last(i):
            k, half = divmod(i, 2)
            if half == 0:
                d5_new = work.tile([P, 2, NB], F32, name="d5")
                pair_root[k] = d5_new
            nc.scalar.activation(
                out=pair_root[k][:, half, :], in_=pair_abs[k][:, half, :],
                func=ACT.Abs_reciprocal_sqrt, bias=one[:],
            )

        def inverse_last(i):
            k, half = divmod(i, 2)
            if half == 0:
                d6_new = work.tile([P, 2, NB], F32, name="d6")
                pair_inv[k] = d6_new
            nc.scalar.activation(
                out=pair_inv[k][:, half, :], in_=pair_root[k][:, half, :], func=ACT.Square
            )
            den[i] = pair_inv[k][:, half, :]

        def inverse(k):
            d6 = work.tile([P, 2, NB], F32, name="d6")
            nc.scalar.activation(out=d6[:], in_=pair_root[k][:], func=ACT.Square)
            den[2 * k] = d6[:, 0, :]
            den[2 * k + 1] = d6[:, 1, :]

        def final_on_gpsimd(i):
            return False

        def numerator(i):
            nb, g, ob = where(i)
            if final_on_gpsimd(i):
                n1 = work.tile([P, NB], F32, name="n1")
                nc.scalar.copy(out=n1[:], in_=n_back[i][:].rearrange("p j o -> p (j o)"))
                n_back[i] = n1

        def divide_and_store(i, on_gpsimd):
            nb, g, ob = where(i)
            if final_on_gpsimd(i) != on_gpsimd:
                return
            m = i // OBS
            if m not in results:
                res_new = work.tile([P, SUB, OBS, P], F32, name="res", bufs=3)
                results[m] = res_new
            res = results[m]
            if on_gpsimd:
                nc.gpsimd.tensor_tensor(
                    out=res[:, :, ob, :],
                    in0=n_back[i][:].rearrange("p (j o) -> p j o", j=SUB),
                    in1=den[i].rearrange("p (j o) -> p j o", j=SUB),
                    op=ALU.mult,
                )
            else:
                nc.vector.tensor_tensor(
                    out=res[:, :, ob, :],
                    in0=n_back[i][:],
                    in1=den[i].rearrange("p (j o) -> p j o", j=SUB),
                    op=ALU.mult,
                )
            rows = out[nb * NB : (nb + 1) * NB, g * GOUT : (g + 1) * GOUT].rearrange(
                "(j r) (k o) -> r j k o", r=P, o=P
            )
            if m == MACROS - 1:
                nc.sync.dma_start(out=rows[:, :, ob, :], in_=res[:, :, ob, :])
            elif ob == OBS - 1:
                nc.sync.dma_start(
                    out=rows.rearrange("r j k o -> r j (k o)"),
                    in_=res[:].rearrange("p j k o -> p j (k o)"),
                )

        def divide_v(i):
            divide_and_store(i, False)

        def divide_g(i):
            divide_and_store(i, True)

        def units_turned_at(t):
            if t in (-2, -1):
                return [2 * t + 8, 2 * t + 9]
            if -4 <= t < 0 or not 0 <= t + 8 < UNITS:
                return []
            return [t + 8]

        def run(stage, i, count=TILES):
            if 0 <= i < count:
                stage(i)

        for t in range(-8, TILES + 6):
            if t == -8:
                quantise_x(0)
            elif (t + 3) % OBS == 0 and t + 3 >= OBS:
                run(quantise_x, (t + 3) // OBS, MACROS)
            run(square_y, t + 1)
            run(outer_terms, t + 1)
            run(quadratics, t)
            run(divide_g, t - 5)
            run(divide_v, t - 5)
            run(product_two, t)
            run(turn_back_q, t - 2)
            run(turn_back_n, t - 4)
            run(magnitude, t - 2)
            for u in units_turned_at(t - 1):
                group_x(u)
                if u < SUB:
                    quantise_unit(u)
            if t % 2 == 1:
                run(inverse_root, (t - 3) // 2, TILES // 2 - 1)
            else:
                run(inverse, (t - 4) // 2, TILES // 2 - 1)
            if t - 2 >= TILES - 2:
                run(inverse_root_last, t - 2)
            if t - 3 >= TILES - 2:
                run(inverse_last, t - 3)
            run(numerator, t - 4)
            if t < 0:
                run(multiply, t + 2)
            for u in units_turned_at(t):
                turn_x(u)
            if t == -5:
                channel_constants()
            if t >= 0:
                run(multiply, t + 2)
            run(load_x, t + 8 + LOADS_AHEAD, UNITS)
